import numpy as np
import ml_dtypes

BF16 = ml_dtypes.bfloat16


def bf(x):
    return np.asarray(x, np.float32).astype(BF16)


def f32(x):
    return np.asarray(x, np.float32)


def f64(x):
    return np.asarray(x).astype(np.float64)


def striped(idx):
    return np.tile(idx.reshape(-1, 16).T, (8, 1))


D, C, S, N = 128, 256, 2048, 512
E_SCALE, P_SCALE, B_SCALE = 1.0 / 32.0, 4.0, 0.25


def setup_inputs():
    return {
        "base": f32(B_SCALE * np.random.standard_normal((C, S))),
        "ed": bf(E_SCALE * np.random.random((N, N))),
        "ei": bf(E_SCALE * np.random.random((N, N))),
        "pn": bf(P_SCALE * np.random.standard_normal((N, D))),
        "offs": striped(np.random.permutation(S)[:N]),
    }


def aggregate(e, p):
    m = e * (1.0 - np.eye(N))
    return (p.T @ m) * (1.0 / m.sum(axis=0, keepdims=True))


def reference(base, ed, ei, pn, offs):
    idx = offs[:16].T.reshape(-1)
    res = f64(base).copy()
    res[:, idx] = np.concatenate([aggregate(f64(ed), f64(pn)), aggregate(f64(ei), f64(pn))], axis=0)
    return res

@@ -1,0 +1,83 @@
+import concourse.mybir as mybir
+from concourse.masks import make_identity
+
+P = 128
+NODES = 512
+STORE = 2048
+BLOCKS = NODES // P
+
+BF16, F32, U16 = mybir.dt.bfloat16, mybir.dt.float32, mybir.dt.uint16
+MULT, NOT_EQUAL = mybir.AluOpType.mult, mybir.AluOpType.not_equal
+COPY = mybir.ActivationFunctionType.Copy
+
+FLOPS = 2 * 2 * P * NODES * NODES
+
+
+def tile_yuyipointupdate_kernel(tc, base, ed, ei, pn, offs, out):
+    nc = tc.nc
+    with tc.tile_pool(name="held", bufs=1) as held, tc.psum_pool(name="banks", bufs=1) as banks:
+        offsets = held.tile([P, NODES // 16], U16, name="offsets")
+        nc.sync.dma_start(offsets[:], offs)
+
+        features = held.tile([P, BLOCKS, P], BF16, name="features")
+        nc.sync.dma_start(features[:], pn.rearrange("(kb p) d -> p kb d", p=P))
+
+        one = held.tile([P, 1], BF16, name="one")
+        nc.gpsimd.memset(one[:], 1.0)
+        identity = held.tile([P, P], F32, name="identity")
+        make_identity(nc, identity[:])
+
+        off_diagonal = held.tile([P, P], BF16, name="off_diagonal")
+        nc.gpsimd.memset(off_diagonal[:], 1.0)
+        nc.gpsimd.affine_select(
+            out=off_diagonal[:],
+            in_=off_diagonal[:],
+            compare_op=NOT_EQUAL,
+            fill=0.0,
+            base=0,
+            pattern=[[-1, P]],
+            channel_multiplier=1,
+        )
+
+        for half, edges_dram in enumerate((ed, ei)):
+            rows = slice(half * P, (half + 1) * P)
+
+            edges = held.tile([P, BLOCKS, NODES], BF16, name=f"edges{half}")
+            nc.scalar.dma_start(edges[:], edges_dram.rearrange("(kb p) j -> p kb j", p=P))
+            window = held.tile([P, STORE], F32, name=f"window{half}")
+            nc.sync.dma_start(window[:], base[rows, :])
+
+            for kb in range(BLOCKS):
+                own = edges[:, kb, kb * P : (kb + 1) * P]
+                nc.vector.tensor_tensor(own, own, off_diagonal[:], MULT)
+
+            weight = banks.tile([P, BLOCKS], F32, name=f"weight{half}")
+            for jb in range(BLOCKS):
+                for kb in range(BLOCKS):
+                    nc.tensor.matmul(
+                        weight[:, jb : jb + 1],
+                        lhsT=edges[:, kb, jb * P : (jb + 1) * P],
+                        rhs=one[:],
+                        start=kb == 0,
+                        stop=kb == BLOCKS - 1,
+                    )
+            inverse = held.tile([P, BLOCKS], F32, name=f"inverse{half}")
+            nc.vector.reciprocal(inverse[:], weight[:])
+
+            summed = banks.tile([P, NODES], F32, name=f"summed{half}")
+            for kb in range(BLOCKS):
+                nc.tensor.matmul(summed[:], lhsT=features[:, kb, :], rhs=edges[:, kb, :], start=kb == 0, stop=kb == BLOCKS - 1)
+
+            spread = banks.tile([P, NODES], F32, name=f"spread{half}")
+            for jb in range(BLOCKS):
+                nc.tensor.transpose(
+                    spread[:, jb * P : (jb + 1) * P], inverse[:, jb : jb + 1].to_broadcast([P, P]), identity[:]
+                )
+
+            numerator = held.tile([P, NODES], F32, name=f"numerator{half}")
+            nc.scalar.activation(numerator[:], summed[:], COPY)
+            reciprocal = held.tile([P, NODES], F32, name=f"reciprocal{half}")
+            nc.scalar.activation(reciprocal[:], spread[:], COPY)
+
+            nc.vector.tensor_tensor(window[:].indirect(offsets[:]), numerator[:], reciprocal[:], MULT)
+            nc.sync.dma_start(out[rows, :], window[:])

@@ -5,28 +5,35 @@ P = 128
 NODES = 512
 STORE = 2048
 BLOCKS = NODES // P
+HALVES = 2
 
 BF16, F32, U16 = mybir.dt.bfloat16, mybir.dt.float32, mybir.dt.uint16
 MULT, NOT_EQUAL = mybir.AluOpType.mult, mybir.AluOpType.not_equal
 COPY = mybir.ActivationFunctionType.Copy
 
-FLOPS = 2 * 2 * P * NODES * NODES
+FLOPS = HALVES * 2 * P * NODES * NODES
 
 
 def tile_yuyipointupdate_kernel(tc, base, ed, ei, pn, offs, out):
     nc = tc.nc
+    queues = (nc.sync, nc.scalar)
     with tc.tile_pool(name="held", bufs=1) as held, tc.psum_pool(name="banks", bufs=1) as banks:
+        features = held.tile([P, BLOCKS, P], BF16, name="features")
+        nc.scalar.dma_start(features[:], pn.rearrange("(kb p) d -> p kb d", p=P))
+        edges = [held.tile([P, BLOCKS, NODES], BF16, name=f"edges{half}") for half in range(HALVES)]
+        for half, edges_dram in enumerate((ed, ei)):
+            for kb in range(BLOCKS):
+                queues[kb % 2].dma_start(edges[half][:, kb, :], edges_dram[kb * P : (kb + 1) * P, :])
         offsets = held.tile([P, NODES // 16], U16, name="offsets")
         nc.sync.dma_start(offsets[:], offs)
-
-        features = held.tile([P, BLOCKS, P], BF16, name="features")
-        nc.sync.dma_start(features[:], pn.rearrange("(kb p) d -> p kb d", p=P))
+        windows = [held.tile([P, STORE], F32, name=f"window{half}") for half in range(HALVES)]
+        for half in range(HALVES):
+            for side, queue in enumerate(queues):
+                columns = slice(side * STORE // 2, (side + 1) * STORE // 2)
+                queue.dma_start(windows[half][:, columns], base[half * P : (half + 1) * P, columns])
 
         one = held.tile([P, 1], BF16, name="one")
         nc.gpsimd.memset(one[:], 1.0)
-        identity = held.tile([P, P], F32, name="identity")
-        make_identity(nc, identity[:])
-
         off_diagonal = held.tile([P, P], BF16, name="off_diagonal")
         nc.gpsimd.memset(off_diagonal[:], 1.0)
         nc.gpsimd.affine_select(
@@ -38,17 +45,14 @@ def tile_yuyipointupdate_kernel(tc, base, ed, ei, pn, offs, out):
             pattern=[[-1, P]],
             channel_multiplier=1,
         )
+        identity = held.tile([P, P], F32, name="identity")
+        make_identity(nc, identity[:])
 
-        for half, edges_dram in enumerate((ed, ei)):
-            rows = slice(half * P, (half + 1) * P)
-
-            edges = held.tile([P, BLOCKS, NODES], BF16, name=f"edges{half}")
-            nc.scalar.dma_start(edges[:], edges_dram.rearrange("(kb p) j -> p kb j", p=P))
-            window = held.tile([P, STORE], F32, name=f"window{half}")
-            nc.sync.dma_start(window[:], base[rows, :])
-
+        numerators = []
+        reciprocals = []
+        for half in range(HALVES):
             for kb in range(BLOCKS):
-                own = edges[:, kb, kb * P : (kb + 1) * P]
+                own = edges[half][:, kb, kb * P : (kb + 1) * P]
                 nc.vector.tensor_tensor(own, own, off_diagonal[:], MULT)
 
             weight = banks.tile([P, BLOCKS], F32, name=f"weight{half}")
@@ -56,7 +60,7 @@ def tile_yuyipointupdate_kernel(tc, base, ed, ei, pn, offs, out):
                 for kb in range(BLOCKS):
                     nc.tensor.matmul(
                         weight[:, jb : jb + 1],
-                        lhsT=edges[:, kb, jb * P : (jb + 1) * P],
+                        lhsT=edges[half][:, kb, jb * P : (jb + 1) * P],
                         rhs=one[:],
                         start=kb == 0,
                         stop=kb == BLOCKS - 1,
@@ -66,18 +70,22 @@ def tile_yuyipointupdate_kernel(tc, base, ed, ei, pn, offs, out):
 
             summed = banks.tile([P, NODES], F32, name=f"summed{half}")
             for kb in range(BLOCKS):
-                nc.tensor.matmul(summed[:], lhsT=features[:, kb, :], rhs=edges[:, kb, :], start=kb == 0, stop=kb == BLOCKS - 1)
+                nc.tensor.matmul(
+                    summed[:], lhsT=features[:, kb, :], rhs=edges[half][:, kb, :], start=kb == 0, stop=kb == BLOCKS - 1
+                )
+            numerator = held.tile([P, NODES], F32, name=f"numerator{half}")
+            nc.scalar.activation(numerator[:], summed[:], COPY)
+            numerators.append(numerator)
 
             spread = banks.tile([P, NODES], F32, name=f"spread{half}")
             for jb in range(BLOCKS):
                 nc.tensor.transpose(
                     spread[:, jb * P : (jb + 1) * P], inverse[:, jb : jb + 1].to_broadcast([P, P]), identity[:]
                 )
-
-            numerator = held.tile([P, NODES], F32, name=f"numerator{half}")
-            nc.scalar.activation(numerator[:], summed[:], COPY)
             reciprocal = held.tile([P, NODES], F32, name=f"reciprocal{half}")
             nc.scalar.activation(reciprocal[:], spread[:], COPY)
+            reciprocals.append(reciprocal)
 
-            nc.vector.tensor_tensor(window[:].indirect(offsets[:]), numerator[:], reciprocal[:], MULT)
-            nc.sync.dma_start(out[rows, :], window[:])
+        for half in range(HALVES):
+            nc.vector.tensor_tensor(windows[half][:].indirect(offsets[:]), numerators[half][:], reciprocals[half][:], MULT)
+            nc.sync.dma_start(out[half * P : (half + 1) * P, :], windows[half][:])

@@ -6,6 +6,7 @@ NODES = 512
 STORE = 2048
 BLOCKS = NODES // P
 HALVES = 2
+WARM_UPS = 4
 
 BF16, F32, U16 = mybir.dt.bfloat16, mybir.dt.float32, mybir.dt.uint16
 MULT, NOT_EQUAL = mybir.AluOpType.mult, mybir.AluOpType.not_equal
@@ -31,6 +32,12 @@ def tile_yuyipointupdate_kernel(tc, base, ed, ei, pn, offs, out):
             for side, queue in enumerate(queues):
                 columns = slice(side * STORE // 2, (side + 1) * STORE // 2)
                 queue.dma_start(windows[half][:, columns], base[half * P : (half + 1) * P, columns])
+
+        zeros = held.tile([P, NODES], BF16, name="zeros")
+        nc.vector.memset(zeros[:], 0.0)
+        unused = banks.tile([P, NODES], F32, name="unused")
+        for repeat in range(WARM_UPS):
+            nc.tensor.matmul(unused[:], lhsT=zeros[:, 0:P], rhs=zeros[:], start=True, stop=True)
 
         one = held.tile([P, 1], BF16, name="one")
         nc.gpsimd.memset(one[:], 1.0)

@@ -17,21 +17,17 @@ FLOPS = HALVES * 2 * P * NODES * NODES
 
 def tile_yuyipointupdate_kernel(tc, base, ed, ei, pn, offs, out):
     nc = tc.nc
-    queues = (nc.sync, nc.scalar)
     with tc.tile_pool(name="held", bufs=1) as held, tc.psum_pool(name="banks", bufs=1) as banks:
         features = held.tile([P, BLOCKS, P], BF16, name="features")
         nc.scalar.dma_start(features[:], pn.rearrange("(kb p) d -> p kb d", p=P))
         edges = [held.tile([P, BLOCKS, NODES], BF16, name=f"edges{half}") for half in range(HALVES)]
         for half, edges_dram in enumerate((ed, ei)):
-            for kb in range(BLOCKS):
-                queues[kb % 2].dma_start(edges[half][:, kb, :], edges_dram[kb * P : (kb + 1) * P, :])
+            nc.sync.dma_start(edges[half][:], edges_dram.rearrange("(kb p) j -> p kb j", p=P))
         offsets = held.tile([P, NODES // 16], U16, name="offsets")
         nc.sync.dma_start(offsets[:], offs)
         windows = [held.tile([P, STORE], F32, name=f"window{half}") for half in range(HALVES)]
         for half in range(HALVES):
-            for side, queue in enumerate(queues):
-                columns = slice(side * STORE // 2, (side + 1) * STORE // 2)
-                queue.dma_start(windows[half][:, columns], base[half * P : (half + 1) * P, columns])
+            nc.sync.dma_start(windows[half][:], base[half * P : (half + 1) * P, :])
 
         zeros = held.tile([P, NODES], BF16, name="zeros")
         nc.vector.memset(zeros[:], 0.0)

@@ -19,15 +19,15 @@ def tile_yuyipointupdate_kernel(tc, base, ed, ei, pn, offs, out):
     nc = tc.nc
     with tc.tile_pool(name="held", bufs=1) as held, tc.psum_pool(name="banks", bufs=1) as banks:
         features = held.tile([P, BLOCKS, P], BF16, name="features")
-        nc.scalar.dma_start(features[:], pn.rearrange("(kb p) d -> p kb d", p=P))
-        edges = [held.tile([P, BLOCKS, NODES], BF16, name=f"edges{half}") for half in range(HALVES)]
-        for half, edges_dram in enumerate((ed, ei)):
-            nc.sync.dma_start(edges[half][:], edges_dram.rearrange("(kb p) j -> p kb j", p=P))
+        nc.sync.dma_start(features[:], pn.rearrange("(kb p) d -> p kb d", p=P))
         offsets = held.tile([P, NODES // 16], U16, name="offsets")
         nc.sync.dma_start(offsets[:], offs)
+        edges = [held.tile([P, BLOCKS, NODES], BF16, name=f"edges{half}") for half in range(HALVES)]
+        for half, edges_dram in enumerate((ed, ei)):
+            nc.scalar.dma_start(edges[half][:], edges_dram.rearrange("(kb p) j -> p kb j", p=P))
         windows = [held.tile([P, STORE], F32, name=f"window{half}") for half in range(HALVES)]
         for half in range(HALVES):
-            nc.sync.dma_start(windows[half][:], base[half * P : (half + 1) * P, :])
+            nc.scalar.dma_start(windows[half][:], base[half * P : (half + 1) * P, :])
 
         zeros = held.tile([P, NODES], BF16, name="zeros")
         nc.vector.memset(zeros[:], 0.0)

@@ -6,7 +6,7 @@ NODES = 512
 STORE = 2048
 BLOCKS = NODES // P
 HALVES = 2
-WARM_UPS = 4
+WARM_UPS = 5
 
 BF16, F32, U16 = mybir.dt.bfloat16, mybir.dt.float32, mybir.dt.uint16
 MULT, NOT_EQUAL = mybir.AluOpType.mult, mybir.AluOpType.not_equal

@@ -10,7 +10,8 @@ WARM_UPS = 5
 
 BF16, F32, U16 = mybir.dt.bfloat16, mybir.dt.float32, mybir.dt.uint16
 MULT, NOT_EQUAL = mybir.AluOpType.mult, mybir.AluOpType.not_equal
-COPY = mybir.ActivationFunctionType.Copy
+COPY, SQUARE = mybir.ActivationFunctionType.Copy, mybir.ActivationFunctionType.Square
+RSQRT = mybir.ActivationFunctionType.Abs_reciprocal_sqrt
 
 FLOPS = HALVES * 2 * P * NODES * NODES
 
@@ -35,8 +36,10 @@ def tile_yuyipointupdate_kernel(tc, base, ed, ei, pn, offs, out):
         for repeat in range(WARM_UPS):
             nc.tensor.matmul(unused[:], lhsT=zeros[:, 0:P], rhs=zeros[:], start=True, stop=True)
 
-        one = held.tile([P, 1], BF16, name="one")
-        nc.gpsimd.memset(one[:], 1.0)
+        ones = held.tile([P, P], BF16, name="ones")
+        nc.gpsimd.memset(ones[:], 1.0)
+        unused_root = held.tile([P, 1], F32, name="unused_root")
+        nc.scalar.activation(unused_root[:], ones[:, 0:1], RSQRT)
         off_diagonal = held.tile([P, P], BF16, name="off_diagonal")
         nc.gpsimd.memset(off_diagonal[:], 1.0)
         nc.gpsimd.affine_select(
@@ -51,43 +54,49 @@ def tile_yuyipointupdate_kernel(tc, base, ed, ei, pn, offs, out):
         identity = held.tile([P, P], F32, name="identity")
         make_identity(nc, identity[:])
 
-        numerators = []
-        reciprocals = []
         for half in range(HALVES):
             for kb in range(BLOCKS):
                 own = edges[half][:, kb, kb * P : (kb + 1) * P]
                 nc.vector.tensor_tensor(own, own, off_diagonal[:], MULT)
 
-            weight = banks.tile([P, BLOCKS], F32, name=f"weight{half}")
-            for jb in range(BLOCKS):
-                for kb in range(BLOCKS):
-                    nc.tensor.matmul(
-                        weight[:, jb : jb + 1],
-                        lhsT=edges[half][:, kb, jb * P : (jb + 1) * P],
-                        rhs=one[:],
-                        start=kb == 0,
-                        stop=kb == BLOCKS - 1,
-                    )
-            inverse = held.tile([P, BLOCKS], F32, name=f"inverse{half}")
-            nc.vector.reciprocal(inverse[:], weight[:])
-
-            summed = banks.tile([P, NODES], F32, name=f"summed{half}")
+        def sum_features(half, tag):
+            summed = banks.tile([P, NODES], F32, name=f"summed{half}", tag=tag)
             for kb in range(BLOCKS):
                 nc.tensor.matmul(
                     summed[:], lhsT=features[:, kb, :], rhs=edges[half][:, kb, :], start=kb == 0, stop=kb == BLOCKS - 1
                 )
             numerator = held.tile([P, NODES], F32, name=f"numerator{half}")
             nc.scalar.activation(numerator[:], summed[:], COPY)
-            numerators.append(numerator)
+            return numerator
 
-            spread = banks.tile([P, NODES], F32, name=f"spread{half}")
-            for jb in range(BLOCKS):
-                nc.tensor.transpose(
-                    spread[:, jb * P : (jb + 1) * P], inverse[:, jb : jb + 1].to_broadcast([P, P]), identity[:]
+        weight = banks.tile([P, BLOCKS], F32, name="weight0", tag="weight")
+        for jb in range(BLOCKS):
+            for kb in range(BLOCKS):
+                nc.tensor.matmul(
+                    weight[:, jb : jb + 1],
+                    lhsT=edges[0][:, kb, jb * P : (jb + 1) * P],
+                    rhs=ones[:, 0:1],
+                    start=kb == 0,
+                    stop=kb == BLOCKS - 1,
                 )
-            reciprocal = held.tile([P, NODES], F32, name=f"reciprocal{half}")
-            nc.scalar.activation(reciprocal[:], spread[:], COPY)
-            reciprocals.append(reciprocal)
+        inverse = held.tile([P, BLOCKS], F32, name="inverse")
+        nc.vector.reciprocal(inverse[:], weight[:])
+        numerators = [sum_features(0, "summed")]
+        spread = banks.tile([P, NODES], F32, name="spread")
+        for jb in range(BLOCKS):
+            nc.tensor.transpose(
+                spread[:, jb * P : (jb + 1) * P], inverse[:, jb : jb + 1].to_broadcast([P, P]), identity[:]
+            )
+        reciprocals = [held.tile([P, NODES], F32, name=f"reciprocal{half}") for half in range(HALVES)]
+        nc.vector.tensor_copy(reciprocals[0][:], spread[:])
+
+        weight = banks.tile([P, NODES], F32, name="weight1", tag="weight")
+        for kb in range(BLOCKS):
+            nc.tensor.matmul(weight[:], lhsT=ones[:], rhs=edges[1][:, kb, :], start=kb == 0, stop=kb == BLOCKS - 1)
+        root = held.tile([P, NODES], F32, name="root")
+        nc.scalar.activation(root[:], weight[:], RSQRT)
+        nc.scalar.activation(reciprocals[1][:], root[:], SQUARE)
+        numerators.append(sum_features(1, "summed"))
 
         for half in range(HALVES):
             nc.vector.tensor_tensor(windows[half][:].indirect(offsets[:]), numerators[half][:], reciprocals[half][:], MULT)

@@ -6,6 +6,9 @@ NODES = 512
 STORE = 2048
 BLOCKS = NODES // P
 HALVES = 2
+SIDES = 2
+SIDE = NODES // SIDES
+SIDE_BLOCKS = SIDE // P
 WARM_UPS = 5
 
 BF16, F32, U16 = mybir.dt.bfloat16, mybir.dt.float32, mybir.dt.uint16
@@ -23,12 +26,29 @@ def tile_yuyipointupdate_kernel(tc, base, ed, ei, pn, offs, out):
         nc.sync.dma_start(features[:], pn.rearrange("(kb p) d -> p kb d", p=P))
         offsets = held.tile([P, NODES // 16], U16, name="offsets")
         nc.sync.dma_start(offsets[:], offs)
-        edges = [held.tile([P, BLOCKS, NODES], BF16, name=f"edges{half}") for half in range(HALVES)]
-        for half, edges_dram in enumerate((ed, ei)):
-            nc.scalar.dma_start(edges[half][:], edges_dram.rearrange("(kb p) j -> p kb j", p=P))
+        edges = []
+        for a in range(SIDES):
+            side = held.tile([P, SIDE_BLOCKS, NODES], BF16, name=f"side{a}")
+            nc.scalar.dma_start(side[:], ed[a * SIDE : (a + 1) * SIDE, :].rearrange("(c p) j -> p c j", p=P))
+            edges.extend(side[:, c, :] for c in range(SIDE_BLOCKS))
+        quadrants = {}
+
+        def load_quadrant(a, b):
+            quadrants[a, b] = held.tile([P, SIDE_BLOCKS, SIDE], BF16, name=f"quadrant{a}{b}")
+            senders = ei[a * SIDE : (a + 1) * SIDE, b * SIDE : (b + 1) * SIDE]
+            nc.scalar.dma_start(quadrants[a, b][:], senders.rearrange("(c p) j -> p c j", p=P))
+
+        load_quadrant(0, 0)
+        load_quadrant(1, 1)
         windows = [held.tile([P, STORE], F32, name=f"window{half}") for half in range(HALVES)]
-        for half in range(HALVES):
-            nc.scalar.dma_start(windows[half][:], base[half * P : (half + 1) * P, :])
+        nc.scalar.dma_start(windows[0][:], base[0:P, :])
+        ones = held.tile([P, P], BF16, name="ones")
+        nc.gpsimd.memset(ones[:], 1.0)
+        unused_root = held.tile([P, 1], F32, name="unused_root")
+        nc.scalar.activation(unused_root[:], ones[:, 0:1], RSQRT)
+        load_quadrant(1, 0)
+        load_quadrant(0, 1)
+        nc.scalar.dma_start(windows[1][:], base[P : 2 * P, :])
 
         zeros = held.tile([P, NODES], BF16, name="zeros")
         nc.vector.memset(zeros[:], 0.0)
@@ -36,10 +56,6 @@ def tile_yuyipointupdate_kernel(tc, base, ed, ei, pn, offs, out):
         for repeat in range(WARM_UPS):
             nc.tensor.matmul(unused[:], lhsT=zeros[:, 0:P], rhs=zeros[:], start=True, stop=True)
 
-        ones = held.tile([P, P], BF16, name="ones")
-        nc.gpsimd.memset(ones[:], 1.0)
-        unused_root = held.tile([P, 1], F32, name="unused_root")
-        nc.scalar.activation(unused_root[:], ones[:, 0:1], RSQRT)
         off_diagonal = held.tile([P, P], BF16, name="off_diagonal")
         nc.gpsimd.memset(off_diagonal[:], 1.0)
         nc.gpsimd.affine_select(
@@ -54,49 +70,67 @@ def tile_yuyipointupdate_kernel(tc, base, ed, ei, pn, offs, out):
         identity = held.tile([P, P], F32, name="identity")
         make_identity(nc, identity[:])
 
-        for half in range(HALVES):
-            for kb in range(BLOCKS):
-                own = edges[half][:, kb, kb * P : (kb + 1) * P]
+        for kb in range(BLOCKS):
+            own = edges[kb][:, kb * P : (kb + 1) * P]
+            nc.vector.tensor_tensor(own, own, off_diagonal[:], MULT)
+        for a in range(SIDES):
+            for c in range(SIDE_BLOCKS):
+                own = quadrants[a, a][:, c, c * P : (c + 1) * P]
                 nc.vector.tensor_tensor(own, own, off_diagonal[:], MULT)
 
-        def sum_features(half, tag):
-            summed = banks.tile([P, NODES], F32, name=f"summed{half}", tag=tag)
-            for kb in range(BLOCKS):
-                nc.tensor.matmul(
-                    summed[:], lhsT=features[:, kb, :], rhs=edges[half][:, kb, :], start=kb == 0, stop=kb == BLOCKS - 1
-                )
-            numerator = held.tile([P, NODES], F32, name=f"numerator{half}")
-            nc.scalar.activation(numerator[:], summed[:], COPY)
-            return numerator
+        numerators = [held.tile([P, NODES], F32, name=f"numerator{half}") for half in range(HALVES)]
+        reciprocals = [held.tile([P, NODES], F32, name=f"reciprocal{half}") for half in range(HALVES)]
 
         weight = banks.tile([P, BLOCKS], F32, name="weight0", tag="weight")
         for jb in range(BLOCKS):
             for kb in range(BLOCKS):
                 nc.tensor.matmul(
                     weight[:, jb : jb + 1],
-                    lhsT=edges[0][:, kb, jb * P : (jb + 1) * P],
+                    lhsT=edges[kb][:, jb * P : (jb + 1) * P],
                     rhs=ones[:, 0:1],
                     start=kb == 0,
                     stop=kb == BLOCKS - 1,
                 )
         inverse = held.tile([P, BLOCKS], F32, name="inverse")
         nc.vector.reciprocal(inverse[:], weight[:])
-        numerators = [sum_features(0, "summed")]
+        summed = banks.tile([P, NODES], F32, name="summed0", tag="summed")
+        for kb in range(BLOCKS):
+            nc.tensor.matmul(
+                summed[:], lhsT=features[:, kb, :], rhs=edges[kb], start=kb == 0, stop=kb == BLOCKS - 1
+            )
+        nc.scalar.activation(numerators[0][:], summed[:], COPY)
         spread = banks.tile([P, NODES], F32, name="spread")
         for jb in range(BLOCKS):
             nc.tensor.transpose(
                 spread[:, jb * P : (jb + 1) * P], inverse[:, jb : jb + 1].to_broadcast([P, P]), identity[:]
             )
-        reciprocals = [held.tile([P, NODES], F32, name=f"reciprocal{half}") for half in range(HALVES)]
         nc.vector.tensor_copy(reciprocals[0][:], spread[:])
 
-        weight = banks.tile([P, NODES], F32, name="weight1", tag="weight")
-        for kb in range(BLOCKS):
-            nc.tensor.matmul(weight[:], lhsT=ones[:], rhs=edges[1][:, kb, :], start=kb == 0, stop=kb == BLOCKS - 1)
-        root = held.tile([P, NODES], F32, name="root")
-        nc.scalar.activation(root[:], weight[:], RSQRT)
-        nc.scalar.activation(reciprocals[1][:], root[:], SQUARE)
-        numerators.append(sum_features(1, "summed"))
+        weights = banks.tile([P, SIDES, NODES], F32, name="weight1", tag="weight")
+        features_summed = banks.tile([P, SIDES, NODES], F32, name="summed1", tag="summed")
+        roots = held.tile([P, NODES], F32, name="roots")
+        for b in range(SIDES):
+            receivers = slice(b * SIDE, (b + 1) * SIDE)
+            blocks = [(a, c) for a in (b, 1 - b) for c in range(SIDE_BLOCKS)]
+            for a, c in blocks:
+                nc.tensor.matmul(
+                    weights[:, b, 0:SIDE],
+                    lhsT=ones[:],
+                    rhs=quadrants[a, b][:, c, :],
+                    start=(a, c) == blocks[0],
+                    stop=(a, c) == blocks[-1],
+                )
+            for a, c in blocks:
+                nc.tensor.matmul(
+                    features_summed[:, b, 0:SIDE],
+                    lhsT=features[:, a * SIDE_BLOCKS + c, :],
+                    rhs=quadrants[a, b][:, c, :],
+                    start=(a, c) == blocks[0],
+                    stop=(a, c) == blocks[-1],
+                )
+            nc.scalar.activation(roots[:, receivers], weights[:, b, 0:SIDE], RSQRT)
+            nc.scalar.activation(reciprocals[1][:, receivers], roots[:, receivers], SQUARE)
+            nc.scalar.activation(numerators[1][:, receivers], features_summed[:, b, 0:SIDE], COPY)
 
         for half in range(HALVES):
             nc.vector.tensor_tensor(windows[half][:].indirect(offsets[:]), numerators[half][:], reciprocals[half][:], MULT)

import concourse.mybir as mybir
from concourse.masks import make_identity

P = 128
NODES = 512
STORE = 2048
BLOCKS = NODES // P
HALVES = 2
SIDES = 2
SIDE = NODES // SIDES
SIDE_BLOCKS = SIDE // P
WARM_UPS = 5

BF16, F32, U16 = mybir.dt.bfloat16, mybir.dt.float32, mybir.dt.uint16
MULT, NOT_EQUAL = mybir.AluOpType.mult, mybir.AluOpType.not_equal
COPY, SQUARE = mybir.ActivationFunctionType.Copy, mybir.ActivationFunctionType.Square
RSQRT = mybir.ActivationFunctionType.Abs_reciprocal_sqrt

FLOPS = HALVES * 2 * P * NODES * NODES


def tile_yuyipointupdate_kernel(tc, base, ed, ei, pn, offs, out):
    nc = tc.nc
    with tc.tile_pool(name="held", bufs=1) as held, tc.psum_pool(name="banks", bufs=1) as banks:
        features = held.tile([P, BLOCKS, P], BF16, name="features")
        nc.sync.dma_start(features[:], pn.rearrange("(kb p) d -> p kb d", p=P))
        offsets = held.tile([P, NODES // 16], U16, name="offsets")
        nc.sync.dma_start(offsets[:], offs)
        edges = []
        for a in range(SIDES):
            side = held.tile([P, SIDE_BLOCKS, NODES], BF16, name=f"side{a}")
            nc.scalar.dma_start(side[:], ed[a * SIDE : (a + 1) * SIDE, :].rearrange("(c p) j -> p c j", p=P))
            edges.extend(side[:, c, :] for c in range(SIDE_BLOCKS))
        quadrants = {}

        def load_quadrant(a, b):
            quadrants[a, b] = held.tile([P, SIDE_BLOCKS, SIDE], BF16, name=f"quadrant{a}{b}")
            senders = ei[a * SIDE : (a + 1) * SIDE, b * SIDE : (b + 1) * SIDE]
            nc.scalar.dma_start(quadrants[a, b][:], senders.rearrange("(c p) j -> p c j", p=P))

        load_quadrant(0, 0)
        load_quadrant(1, 1)
        windows = [held.tile([P, STORE], F32, name=f"window{half}") for half in range(HALVES)]
        nc.scalar.dma_start(windows[0][:], base[0:P, :])
        ones = held.tile([P, P], BF16, name="ones")
        nc.gpsimd.memset(ones[:], 1.0)
        unused_root = held.tile([P, 1], F32, name="unused_root")
        nc.scalar.activation(unused_root[:], ones[:, 0:1], RSQRT)
        load_quadrant(1, 0)
        load_quadrant(0, 1)
        nc.scalar.dma_start(windows[1][:], base[P : 2 * P, :])

        zeros = held.tile([P, NODES], BF16, name="zeros")
        nc.vector.memset(zeros[:], 0.0)
        unused = banks.tile([P, NODES], F32, name="unused")
        for repeat in range(WARM_UPS):
            nc.tensor.matmul(unused[:], lhsT=zeros[:, 0:P], rhs=zeros[:], start=True, stop=True)

        off_diagonal = held.tile([P, P], BF16, name="off_diagonal")
        nc.gpsimd.memset(off_diagonal[:], 1.0)
        nc.gpsimd.affine_select(
            out=off_diagonal[:],
            in_=off_diagonal[:],
            compare_op=NOT_EQUAL,
            fill=0.0,
            base=0,
            pattern=[[-1, P]],
            channel_multiplier=1,
        )
        identity = held.tile([P, P], F32, name="identity")
        make_identity(nc, identity[:])

        for kb in range(BLOCKS):
            own = edges[kb][:, kb * P : (kb + 1) * P]
            nc.vector.tensor_tensor(own, own, off_diagonal[:], MULT)
        for a in range(SIDES):
            for c in range(SIDE_BLOCKS):
                own = quadrants[a, a][:, c, c * P : (c + 1) * P]
                nc.vector.tensor_tensor(own, own, off_diagonal[:], MULT)

        numerators = [held.tile([P, NODES], F32, name=f"numerator{half}") for half in range(HALVES)]
        reciprocals = [held.tile([P, NODES], F32, name=f"reciprocal{half}") for half in range(HALVES)]

        weight = banks.tile([P, BLOCKS], F32, name="weight0", tag="weight")
        for jb in range(BLOCKS):
            for kb in range(BLOCKS):
                nc.tensor.matmul(
                    weight[:, jb : jb + 1],
                    lhsT=edges[kb][:, jb * P : (jb + 1) * P],
                    rhs=ones[:, 0:1],
                    start=kb == 0,
                    stop=kb == BLOCKS - 1,
                )
        inverse = held.tile([P, BLOCKS], F32, name="inverse")
        nc.vector.reciprocal(inverse[:], weight[:])
        summed = banks.tile([P, NODES], F32, name="summed0", tag="summed")
        for kb in range(BLOCKS):
            nc.tensor.matmul(
                summed[:], lhsT=features[:, kb, :], rhs=edges[kb], start=kb == 0, stop=kb == BLOCKS - 1
            )
        nc.scalar.activation(numerators[0][:], summed[:], COPY)
        spread = banks.tile([P, NODES], F32, name="spread")
        for jb in range(BLOCKS):
            nc.tensor.transpose(
                spread[:, jb * P : (jb + 1) * P], inverse[:, jb : jb + 1].to_broadcast([P, P]), identity[:]
            )
        nc.vector.tensor_copy(reciprocals[0][:], spread[:])

        weights = banks.tile([P, SIDES, NODES], F32, name="weight1", tag="weight")
        features_summed = banks.tile([P, SIDES, NODES], F32, name="summed1", tag="summed")
        roots = held.tile([P, NODES], F32, name="roots")
        for b in range(SIDES):
            receivers = slice(b * SIDE, (b + 1) * SIDE)
            blocks = [(a, c) for a in (b, 1 - b) for c in range(SIDE_BLOCKS)]
            for a, c in blocks:
                nc.tensor.matmul(
                    weights[:, b, 0:SIDE],
                    lhsT=ones[:],
                    rhs=quadrants[a, b][:, c, :],
                    start=(a, c) == blocks[0],
                    stop=(a, c) == blocks[-1],
                )
            for a, c in blocks:
                nc.tensor.matmul(
                    features_summed[:, b, 0:SIDE],
                    lhsT=features[:, a * SIDE_BLOCKS + c, :],
                    rhs=quadrants[a, b][:, c, :],
                    start=(a, c) == blocks[0],
                    stop=(a, c) == blocks[-1],
                )
            nc.scalar.activation(roots[:, receivers], weights[:, b, 0:SIDE], RSQRT)
            nc.scalar.activation(reciprocals[1][:, receivers], roots[:, receivers], SQUARE)
            nc.scalar.activation(numerators[1][:, receivers], features_summed[:, b, 0:SIDE], COPY)

        for half in range(HALVES):
            nc.vector.tensor_tensor(windows[half][:].indirect(offsets[:]), numerators[half][:], reciprocals[half][:], MULT)
            nc.sync.dma_start(out[half * P : (half + 1) * P, :], windows[half][:])
